import numpy as np
import ml_dtypes

BF16 = ml_dtypes.bfloat16


def bf(x):
    return np.asarray(x, np.float32).astype(BF16)


def f32(x):
    return np.asarray(x, np.float32)


def f64(x):
    return np.asarray(x).astype(np.float64)


def striped(idx):
    return np.tile(idx.reshape(-1, 16).T, (8, 1))


D, S, K, M, N, H = 128, 1024, 4, 256, 4096, 512
SLOPE = 0.2


def setup_inputs():
    x = bf(np.random.standard_normal((D, S)))
    wa = bf(np.random.standard_normal((D, M)) / np.sqrt(2.0 * D))
    wb = bf(np.random.standard_normal((D, M)) / np.sqrt(2.0 * D))
    b = f32(0.1 * np.random.standard_normal((M, 1)))
    idx = np.concatenate([np.random.permutation(S)[:H] for _ in range(N // H)])
    return {"x": x, "wa": wa, "wb": wb, "b": b, "offs": striped(idx)}


def reference(x, wa, wb, b, offs):
    idx = offs[:16].T.reshape(-1)
    xs = f64(x)
    nb = (f64(wa).T @ xs[:, idx]).reshape(M, K, S)
    ctr = f64(wb).T @ xs - f64(wa).T @ xs + f64(b)
    h = nb + ctr[:, None, :]
    return np.maximum(h, SLOPE * h).max(axis=1)

@@ -1,0 +1,113 @@
+import concourse.mybir as mybir
+
+BF16, F32, U16 = mybir.dt.bfloat16, mybir.dt.float32, mybir.dt.uint16
+ADD, MULT, MAX = mybir.AluOpType.add, mybir.AluOpType.mult, mybir.AluOpType.max
+RELU = mybir.ActivationFunctionType.Relu
+
+P = 128
+NODES = 1024
+FEATURES = 256
+NEIGHBOURS = 4
+SLOPE = 0.2
+PIECE = 512
+HALVES = NODES // PIECE
+BLOCKS = FEATURES // P
+PSUM_BANKS = 8
+CUTS = 2
+WARM_UP = 8
+
+FLOPS = 2 * P * FEATURES * (NEIGHBOURS * NODES + 2 * NODES)
+
+
+def tile_skeletonconv_kernel(tc, x, wa, wb, b, offs, out):
+    nc = tc.nc
+    cols = PIECE // 16
+
+    with (
+        tc.tile_pool(name="held", bufs=1) as held,
+        tc.tile_pool(name="work", bufs=HALVES) as work,
+        tc.psum_pool(name="psum", bufs=PSUM_BANKS) as psum,
+    ):
+        offsets = held.tile([P, NEIGHBOURS * NODES // 16], U16, name="offsets")
+        nodes = held.tile([P, NODES], BF16, name="nodes")
+        wa_sb = held.tile([P, FEATURES], BF16, name="wa_sb")
+        wb_sb = held.tile([P, FEATURES], BF16, name="wb_sb")
+        bias = [held.tile([P, 1], F32, name=f"bias{f}") for f in range(BLOCKS)]
+        nc.sync.dma_start(nodes[:, :PIECE], x[:, :PIECE])
+        nc.scalar.dma_start(wb_sb[:], wb)
+        nc.sync.dma_start(wa_sb[:], wa)
+        nc.sync.dma_start(nodes[:, PIECE:], x[:, PIECE:])
+        nc.sync.dma_start(offsets[:], offs)
+        for f in range(BLOCKS):
+            nc.scalar.dma_start(bias[f][:], b[f * P : (f + 1) * P, :])
+
+        zeros = held.tile([P, P], BF16, name="zeros")
+        nc.vector.memset(zeros[:], 0.0)
+        warm_up = psum.tile([P, P], F32, name="warm_up", tag="bank")
+        for i in range(WARM_UP):
+            nc.tensor.matmul(warm_up[:], zeros[:], zeros[:], start=True, stop=True)
+
+        wa_neg = held.tile([P, FEATURES], BF16, name="wa_neg")
+        nc.vector.tensor_scalar_mul(wa_neg[:], wa_sb[:], -1.0)
+
+        def centre_terms(h):
+            here = nodes[:, h * PIECE : (h + 1) * PIECE]
+            centres = [psum.tile([P, PIECE], F32, name=f"centre{f}", tag="bank") for f in range(BLOCKS)]
+            for f in range(BLOCKS):
+                nc.tensor.matmul(centres[f][:], wb_sb[:, f * P : (f + 1) * P], here, start=True, stop=False)
+            for f in range(BLOCKS):
+                nc.tensor.matmul(centres[f][:], wa_neg[:, f * P : (f + 1) * P], here, start=False, stop=True)
+            return centres
+
+        def best_neighbours(h):
+            bests = [work.tile([P, PIECE], F32, name=f"best{f}") for f in range(BLOCKS)]
+            for k in range(NEIGHBOURS):
+                piece = k * HALVES + h
+                for f in range(BLOCKS):
+                    product = psum.tile([P, PIECE], F32, name="product", tag="bank")
+                    nc.tensor.matmul(
+                        product[:],
+                        wa_sb[:, f * P : (f + 1) * P],
+                        nodes[:].indirect(offsets[:, piece * cols : (piece + 1) * cols]),
+                        start=True,
+                        stop=True,
+                    )
+                    if k == 0:
+                        nc.scalar.copy(bests[f][:], product[:])
+                    else:
+                        nc.vector.tensor_tensor(bests[f][:], product[:], bests[f][:], MAX)
+            return bests
+
+        def add_centres(centres, bests):
+            sums = [work.tile([P, PIECE], F32, name=f"summed{f}") for f in range(BLOCKS)]
+            for f in range(BLOCKS):
+                nc.vector.scalar_tensor_tensor(sums[f][:], centres[f][:], bias[f][:], bests[f][:], ADD, ADD)
+            return sums
+
+        def store(queue, f, h, result):
+            queue.dma_start(out[f * P : (f + 1) * P, h * PIECE : (h + 1) * PIECE], result[:])
+
+        def leaky(h, sums):
+            width = PIECE // CUTS
+            queues = (nc.sync, nc.scalar)
+            for f in range(BLOCKS):
+                result = work.tile([P, PIECE], F32, name=f"result{f}")
+                for c in range(CUTS):
+                    cut = slice(c * width, (c + 1) * width)
+                    nc.vector.scalar_tensor_tensor(result[:, cut], sums[f][:, cut], SLOPE, sums[f][:, cut], MULT, MAX)
+                    queues[c % 2].dma_start(
+                        out[f * P : (f + 1) * P, h * PIECE + cut.start : h * PIECE + cut.stop], result[:, cut]
+                    )
+
+        def leaky_aside(h, sums):
+            for f in range(BLOCKS):
+                lift = work.tile([P, PIECE], F32, name=f"lift{f}")
+                nc.scalar.activation(lift[:], sums[f][:], RELU, scale=SLOPE - 1.0)
+                result = work.tile([P, PIECE], F32, name=f"result{f}")
+                nc.gpsimd.tensor_tensor(result[:], sums[f][:], lift[:], ADD)
+                store(nc.sync, f, h, result)
+
+        sums_first = add_centres(centre_terms(0), best_neighbours(0))
+        bests_second = best_neighbours(1)
+        leaky_aside(0, sums_first)
+        leaky(1, add_centres(centre_terms(1), bests_second))

@@ -47,16 +47,18 @@ def tile_skeletonconv_kernel(tc, x, wa, wb, b, offs, out):
         for i in range(WARM_UP):
             nc.tensor.matmul(warm_up[:], zeros[:], zeros[:], start=True, stop=True)
 
-        wa_neg = held.tile([P, FEATURES], BF16, name="wa_neg")
-        nc.vector.tensor_scalar_mul(wa_neg[:], wa_sb[:], -1.0)
+        nodes_neg = held.tile([P, NODES], BF16, name="nodes_neg")
+        for h in range(HALVES):
+            half = slice(h * PIECE, (h + 1) * PIECE)
+            nc.vector.tensor_scalar_mul(nodes_neg[:, half], nodes[:, half], -1.0)
 
         def centre_terms(h):
-            here = nodes[:, h * PIECE : (h + 1) * PIECE]
+            half = slice(h * PIECE, (h + 1) * PIECE)
             centres = [psum.tile([P, PIECE], F32, name=f"centre{f}", tag="bank") for f in range(BLOCKS)]
             for f in range(BLOCKS):
-                nc.tensor.matmul(centres[f][:], wb_sb[:, f * P : (f + 1) * P], here, start=True, stop=False)
+                nc.tensor.matmul(centres[f][:], wb_sb[:, f * P : (f + 1) * P], nodes[:, half], start=True, stop=False)
             for f in range(BLOCKS):
-                nc.tensor.matmul(centres[f][:], wa_neg[:, f * P : (f + 1) * P], here, start=False, stop=True)
+                nc.tensor.matmul(centres[f][:], wa_sb[:, f * P : (f + 1) * P], nodes_neg[:, half], start=False, stop=True)
             return centres
 
         def best_neighbours(h):

import concourse.mybir as mybir

BF16, F32, U16 = mybir.dt.bfloat16, mybir.dt.float32, mybir.dt.uint16
ADD, MULT, MAX = mybir.AluOpType.add, mybir.AluOpType.mult, mybir.AluOpType.max
RELU = mybir.ActivationFunctionType.Relu

P = 128
NODES = 1024
FEATURES = 256
NEIGHBOURS = 4
SLOPE = 0.2
PIECE = 512
HALVES = NODES // PIECE
BLOCKS = FEATURES // P
PSUM_BANKS = 8
CUTS = 2
WARM_UP = 8

FLOPS = 2 * P * FEATURES * (NEIGHBOURS * NODES + 2 * NODES)


def tile_skeletonconv_kernel(tc, x, wa, wb, b, offs, out):
    nc = tc.nc
    cols = PIECE // 16

    with (
        tc.tile_pool(name="held", bufs=1) as held,
        tc.tile_pool(name="work", bufs=HALVES) as work,
        tc.psum_pool(name="psum", bufs=PSUM_BANKS) as psum,
    ):
        offsets = held.tile([P, NEIGHBOURS * NODES // 16], U16, name="offsets")
        nodes = held.tile([P, NODES], BF16, name="nodes")
        wa_sb = held.tile([P, FEATURES], BF16, name="wa_sb")
        wb_sb = held.tile([P, FEATURES], BF16, name="wb_sb")
        bias = [held.tile([P, 1], F32, name=f"bias{f}") for f in range(BLOCKS)]
        nc.sync.dma_start(nodes[:, :PIECE], x[:, :PIECE])
        nc.scalar.dma_start(wb_sb[:], wb)
        nc.sync.dma_start(wa_sb[:], wa)
        nc.sync.dma_start(nodes[:, PIECE:], x[:, PIECE:])
        nc.sync.dma_start(offsets[:], offs)
        for f in range(BLOCKS):
            nc.scalar.dma_start(bias[f][:], b[f * P : (f + 1) * P, :])

        zeros = held.tile([P, P], BF16, name="zeros")
        nc.vector.memset(zeros[:], 0.0)
        warm_up = psum.tile([P, P], F32, name="warm_up", tag="bank")
        for i in range(WARM_UP):
            nc.tensor.matmul(warm_up[:], zeros[:], zeros[:], start=True, stop=True)

        nodes_neg = held.tile([P, NODES], BF16, name="nodes_neg")
        for h in range(HALVES):
            half = slice(h * PIECE, (h + 1) * PIECE)
            nc.vector.tensor_scalar_mul(nodes_neg[:, half], nodes[:, half], -1.0)

        def centre_terms(h):
            half = slice(h * PIECE, (h + 1) * PIECE)
            centres = [psum.tile([P, PIECE], F32, name=f"centre{f}", tag="bank") for f in range(BLOCKS)]
            for f in range(BLOCKS):
                nc.tensor.matmul(centres[f][:], wb_sb[:, f * P : (f + 1) * P], nodes[:, half], start=True, stop=False)
            for f in range(BLOCKS):
                nc.tensor.matmul(centres[f][:], wa_sb[:, f * P : (f + 1) * P], nodes_neg[:, half], start=False, stop=True)
            return centres

        def best_neighbours(h):
            bests = [work.tile([P, PIECE], F32, name=f"best{f}") for f in range(BLOCKS)]
            for k in range(NEIGHBOURS):
                piece = k * HALVES + h
                for f in range(BLOCKS):
                    product = psum.tile([P, PIECE], F32, name="product", tag="bank")
                    nc.tensor.matmul(
                        product[:],
                        wa_sb[:, f * P : (f + 1) * P],
                        nodes[:].indirect(offsets[:, piece * cols : (piece + 1) * cols]),
                        start=True,
                        stop=True,
                    )
                    if k == 0:
                        nc.scalar.copy(bests[f][:], product[:])
                    else:
                        nc.vector.tensor_tensor(bests[f][:], product[:], bests[f][:], MAX)
            return bests

        def add_centres(centres, bests):
            sums = [work.tile([P, PIECE], F32, name=f"summed{f}") for f in range(BLOCKS)]
            for f in range(BLOCKS):
                nc.vector.scalar_tensor_tensor(sums[f][:], centres[f][:], bias[f][:], bests[f][:], ADD, ADD)
            return sums

        def store(queue, f, h, result):
            queue.dma_start(out[f * P : (f + 1) * P, h * PIECE : (h + 1) * PIECE], result[:])

        def leaky(h, sums):
            width = PIECE // CUTS
            queues = (nc.sync, nc.scalar)
            for f in range(BLOCKS):
                result = work.tile([P, PIECE], F32, name=f"result{f}")
                for c in range(CUTS):
                    cut = slice(c * width, (c + 1) * width)
                    nc.vector.scalar_tensor_tensor(result[:, cut], sums[f][:, cut], SLOPE, sums[f][:, cut], MULT, MAX)
                    queues[c % 2].dma_start(
                        out[f * P : (f + 1) * P, h * PIECE + cut.start : h * PIECE + cut.stop], result[:, cut]
                    )

        def leaky_aside(h, sums):
            for f in range(BLOCKS):
                lift = work.tile([P, PIECE], F32, name=f"lift{f}")
                nc.scalar.activation(lift[:], sums[f][:], RELU, scale=SLOPE - 1.0)
                result = work.tile([P, PIECE], F32, name=f"result{f}")
                nc.gpsimd.tensor_tensor(result[:], sums[f][:], lift[:], ADD)
                store(nc.sync, f, h, result)

        sums_first = add_centres(centre_terms(0), best_neighbours(0))
        bests_second = best_neighbours(1)
        leaky_aside(0, sums_first)
        leaky(1, add_centres(centre_terms(1), bests_second))
